import numpy as np
import ml_dtypes

BF16 = ml_dtypes.bfloat16


def bf(x):
    return np.asarray(x, np.float32).astype(BF16)


def f32(x):
    return np.asarray(x, np.float32)


def f64(x):
    return np.asarray(x).astype(np.float64)


def striped(idx):
    return np.tile(idx.reshape(-1, 16).T, (8, 1))


V, D, B, L, N = 4096, 128, 16, 32, 512


def setup_inputs():
    xav = np.sqrt(6.0 / (D + D))
    return {"table": bf(0.3 * np.random.standard_normal((V, D))), "w": bf(4.5 * np.random.uniform(-xav, xav, (D, D))), "offs": striped(np.random.permutation(np.tile(np.arange(V), 2))[:N])}


def reference(table, w, offs):
    idx = offs[:16].T.reshape(-1)
    x = f64(table)[idx].T
    y = f64(w).T @ x
    xs = x.reshape(D, B, L)
    avg = xs.mean(axis=2)
    score = (y.reshape(D, B, L) * avg[:, :, None]).sum(axis=0)
    e = np.exp(score - score.max(axis=1, keepdims=True))
    a = e / e.sum(axis=1, keepdims=True)
    return (xs * a[None, :, :]).sum(axis=2)

@@ -1,0 +1,83 @@
+import concourse.mybir as mybir
+from concourse.masks import make_identity
+
+BF16, F32, U16 = mybir.dt.bfloat16, mybir.dt.float32, mybir.dt.uint16
+ALU = mybir.AluOpType
+X_AXIS = mybir.AxisListType.X
+EXP = mybir.ActivationFunctionType.Exp
+
+P = 128
+V, D = 4096, 128
+B, L = 16, 32
+N = B * L
+BLOCKS_PER_BANK = 8
+BANKS = V // (P * BLOCKS_PER_BANK)
+PART = P * BLOCKS_PER_BANK
+
+FLOPS = 2 * D * D * N + 4 * D * N
+
+
+def tile_student_hyp_rec_kernel(tc, table, w, offs, out):
+    nc = tc.nc
+    with (
+        tc.tile_pool(name="held", bufs=1) as held,
+        tc.tile_pool(name="rows", bufs=BANKS) as rows_pool,
+        tc.psum_pool(name="flip", bufs=2) as flip_pool,
+        tc.psum_pool(name="banks", bufs=1) as banks,
+    ):
+        offsets = held.tile([P, N // 16], U16, name="offsets")
+        nc.sync.dma_start(offsets[:], offs)
+        weights = held.tile([D, D], BF16, name="weights")
+        nc.scalar.dma_start(weights[:], w)
+
+        identity = held.tile([P, P], BF16, name="identity")
+        make_identity(nc, identity[:])
+        mean_weights = held.tile([D, P], BF16, name="mean_weights")
+        nc.vector.memset(mean_weights[:], 1.0 / L)
+
+        table_blocks = table.rearrange("(k p) d -> p k d", p=P)
+        table_cols = held.tile([D, V], BF16, name="table_cols")
+        for g in range(BANKS):
+            rows = rows_pool.tile([P, BLOCKS_PER_BANK, D], BF16, name="rows")
+            nc.sync.dma_start(rows[:], table_blocks[:, g * BLOCKS_PER_BANK : (g + 1) * BLOCKS_PER_BANK, :])
+            flipped = flip_pool.tile([D, PART], BF16, name="flipped")
+            for k in range(BLOCKS_PER_BANK):
+                nc.tensor.transpose(flipped[:, k * P : (k + 1) * P], rows[:, k, :], identity[:])
+            part_cols = table_cols[:, g * PART : (g + 1) * PART]
+            if g % 2 == 0:
+                nc.vector.tensor_copy(part_cols, flipped[:])
+            else:
+                nc.scalar.copy(part_cols, flipped[:])
+
+        x_bank = banks.tile([D, N], F32, name="x_bank")
+        nc.tensor.matmul(x_bank[:], identity[:], table_cols[:].indirect(offsets[:]), start=True, stop=True)
+        y_bank = banks.tile([D, N], F32, name="y_bank")
+        nc.tensor.matmul(y_bank[:], weights[:], table_cols[:].indirect(offsets[:]), start=True, stop=True)
+        x_words = x_bank[:].rearrange("d (b l) -> d b l", l=L)
+        y_words = y_bank[:].rearrange("d (b l) -> d b l", l=L)
+
+        word_sum = held.tile([D, B], F32, name="word_sum")
+        nc.vector.reduce_sum(word_sum[:], x_words, axis=X_AXIS)
+        products = held.tile([D, B, L], BF16, name="products")
+        nc.vector.tensor_tensor(products[:], y_words, word_sum[:].unsqueeze(2).to_broadcast([D, B, L]), ALU.mult)
+        score_bank = banks.tile([P, N], F32, name="score_bank")
+        nc.tensor.matmul(score_bank[:], mean_weights[:], products[:].rearrange("d b l -> d (b l)"), start=True, stop=True)
+        scores = score_bank[:].rearrange("p (b l) -> p b l", l=L)
+
+        top = held.tile([P, B], F32, name="top")
+        nc.vector.reduce_max(top[:], scores, axis=X_AXIS)
+        shifted = held.tile([P, B, L], F32, name="shifted")
+        nc.vector.tensor_tensor(shifted[:], scores, top[:].unsqueeze(2).to_broadcast([P, B, L]), ALU.subtract)
+        grown = held.tile([P, B, L], F32, name="grown")
+        nc.scalar.activation(grown[:], shifted[:], EXP)
+        denominator = held.tile([P, B], F32, name="denominator")
+        nc.vector.reduce_sum(denominator[:], grown[:], axis=X_AXIS)
+        weighted = held.tile([D, B, L], F32, name="weighted")
+        nc.vector.tensor_tensor(weighted[:], x_words, grown[:], ALU.mult)
+        numerator = held.tile([D, B], F32, name="numerator")
+        nc.vector.reduce_sum(numerator[:], weighted[:], axis=X_AXIS)
+        inverse = held.tile([P, B], F32, name="inverse")
+        nc.vector.reciprocal(inverse[:], denominator[:])
+        result = held.tile([D, B], F32, name="result")
+        nc.vector.tensor_tensor(result[:], numerator[:], inverse[:], ALU.mult)
+        nc.sync.dma_start(out, result[:])

@@ -10,9 +10,9 @@ P = 128
 V, D = 4096, 128
 B, L = 16, 32
 N = B * L
-BLOCKS_PER_BANK = 8
-BANKS = V // (P * BLOCKS_PER_BANK)
-PART = P * BLOCKS_PER_BANK
+PART_BLOCKS = 4
+PART = P * PART_BLOCKS
+PARTS = V // PART
 
 FLOPS = 2 * D * D * N + 4 * D * N
 
@@ -21,33 +21,41 @@ def tile_student_hyp_rec_kernel(tc, table, w, offs, out):
     nc = tc.nc
     with (
         tc.tile_pool(name="held", bufs=1) as held,
-        tc.tile_pool(name="rows", bufs=BANKS) as rows_pool,
-        tc.psum_pool(name="flip", bufs=2) as flip_pool,
+        tc.tile_pool(name="rows", bufs=PARTS) as rows_pool,
+        tc.psum_pool(name="flip", bufs=4) as flip_pool,
         tc.psum_pool(name="banks", bufs=1) as banks,
     ):
+        table_blocks = table.rearrange("(k p) d -> p k d", p=P)
+        parts = []
+        for g in range(PARTS):
+            rows = rows_pool.tile([P, PART_BLOCKS, D], BF16, name="rows")
+            queue = nc.sync if g % 2 == 0 else nc.scalar
+            queue.dma_start(rows[:], table_blocks[:, g * PART_BLOCKS : (g + 1) * PART_BLOCKS, :])
+            parts.append(rows)
         offsets = held.tile([P, N // 16], U16, name="offsets")
         nc.sync.dma_start(offsets[:], offs)
         weights = held.tile([D, D], BF16, name="weights")
-        nc.scalar.dma_start(weights[:], w)
+        nc.gpsimd.dma_start(weights[:], w)
+
+        scratch = held.tile([P, 1], F32, name="scratch")
+        nc.vector.memset(scratch[:], 0.0)
+        nc.scalar.activation(scratch[:], scratch[:], EXP)
 
         identity = held.tile([P, P], BF16, name="identity")
         make_identity(nc, identity[:])
         mean_weights = held.tile([D, P], BF16, name="mean_weights")
         nc.vector.memset(mean_weights[:], 1.0 / L)
 
-        table_blocks = table.rearrange("(k p) d -> p k d", p=P)
         table_cols = held.tile([D, V], BF16, name="table_cols")
-        for g in range(BANKS):
-            rows = rows_pool.tile([P, BLOCKS_PER_BANK, D], BF16, name="rows")
-            nc.sync.dma_start(rows[:], table_blocks[:, g * BLOCKS_PER_BANK : (g + 1) * BLOCKS_PER_BANK, :])
+        for g in range(PARTS):
             flipped = flip_pool.tile([D, PART], BF16, name="flipped")
-            for k in range(BLOCKS_PER_BANK):
-                nc.tensor.transpose(flipped[:, k * P : (k + 1) * P], rows[:, k, :], identity[:])
+            for k in range(PART_BLOCKS):
+                nc.tensor.transpose(flipped[:, k * P : (k + 1) * P], parts[g][:, k, :], identity[:])
             part_cols = table_cols[:, g * PART : (g + 1) * PART]
             if g % 2 == 0:
-                nc.vector.tensor_copy(part_cols, flipped[:])
-            else:
                 nc.scalar.copy(part_cols, flipped[:])
+            else:
+                nc.vector.tensor_copy(part_cols, flipped[:])
 
         x_bank = banks.tile([D, N], F32, name="x_bank")
         nc.tensor.matmul(x_bank[:], identity[:], table_cols[:].indirect(offsets[:]), start=True, stop=True)

@@ -13,6 +13,10 @@ N = B * L
 PART_BLOCKS = 4
 PART = P * PART_BLOCKS
 PARTS = V // PART
+PIECES = 2
+PIECE_B = B // PIECES
+PIECE_N = N // PIECES
+PIECE_COLS = PIECE_N // 16
 
 FLOPS = 2 * D * D * N + 4 * D * N
 
@@ -22,10 +26,11 @@ def tile_student_hyp_rec_kernel(tc, table, w, offs, out):
     with (
         tc.tile_pool(name="held", bufs=1) as held,
         tc.tile_pool(name="rows", bufs=PARTS) as rows_pool,
-        tc.psum_pool(name="flip", bufs=4) as flip_pool,
-        tc.psum_pool(name="banks", bufs=1) as banks,
+        tc.tile_pool(name="work", bufs=PIECES) as work,
     ):
         table_blocks = table.rearrange("(k p) d -> p k d", p=P)
+        weights = held.tile([D, D], BF16, name="weights")
+        nc.scalar.dma_start(weights[:], w)
         parts = []
         for g in range(PARTS):
             rows = rows_pool.tile([P, PART_BLOCKS, D], BF16, name="rows")
@@ -34,8 +39,6 @@ def tile_student_hyp_rec_kernel(tc, table, w, offs, out):
             parts.append(rows)
         offsets = held.tile([P, N // 16], U16, name="offsets")
         nc.sync.dma_start(offsets[:], offs)
-        weights = held.tile([D, D], BF16, name="weights")
-        nc.gpsimd.dma_start(weights[:], w)
 
         scratch = held.tile([P, 1], F32, name="scratch")
         nc.vector.memset(scratch[:], 0.0)
@@ -47,45 +50,64 @@ def tile_student_hyp_rec_kernel(tc, table, w, offs, out):
         nc.vector.memset(mean_weights[:], 1.0 / L)
 
         table_cols = held.tile([D, V], BF16, name="table_cols")
-        for g in range(PARTS):
-            flipped = flip_pool.tile([D, PART], BF16, name="flipped")
-            for k in range(PART_BLOCKS):
-                nc.tensor.transpose(flipped[:, k * P : (k + 1) * P], parts[g][:, k, :], identity[:])
-            part_cols = table_cols[:, g * PART : (g + 1) * PART]
-            if g % 2 == 0:
-                nc.scalar.copy(part_cols, flipped[:])
-            else:
-                nc.vector.tensor_copy(part_cols, flipped[:])
+        with tc.psum_pool(name="flip", bufs=4) as flip_pool:
+            for g in range(PARTS):
+                flipped = flip_pool.tile([D, PART], BF16, name="flipped")
+                for k in range(PART_BLOCKS):
+                    nc.tensor.transpose(flipped[:, k * P : (k + 1) * P], parts[g][:, k, :], identity[:])
+                part_cols = table_cols[:, g * PART : (g + 1) * PART]
+                if g % 2 == 0:
+                    nc.scalar.copy(part_cols, flipped[:])
+                else:
+                    nc.vector.tensor_copy(part_cols, flipped[:])
 
-        x_bank = banks.tile([D, N], F32, name="x_bank")
-        nc.tensor.matmul(x_bank[:], identity[:], table_cols[:].indirect(offsets[:]), start=True, stop=True)
-        y_bank = banks.tile([D, N], F32, name="y_bank")
-        nc.tensor.matmul(y_bank[:], weights[:], table_cols[:].indirect(offsets[:]), start=True, stop=True)
-        x_words = x_bank[:].rearrange("d (b l) -> d b l", l=L)
-        y_words = y_bank[:].rearrange("d (b l) -> d b l", l=L)
+        with tc.psum_pool(name="banks", bufs=PIECES) as banks:
+            x_words, y_words = [], []
+            for h in range(PIECES):
+                piece = offsets[:, h * PIECE_COLS : (h + 1) * PIECE_COLS]
+                x_bank = banks.tile([D, PIECE_N], F32, name="x_bank")
+                nc.tensor.matmul(x_bank[:], identity[:], table_cols[:].indirect(piece), start=True, stop=True)
+                y_bank = banks.tile([D, PIECE_N], F32, name="y_bank")
+                nc.tensor.matmul(y_bank[:], weights[:], table_cols[:].indirect(piece), start=True, stop=True)
+                x_words.append(x_bank[:].rearrange("d (b l) -> d b l", l=L))
+                y_words.append(y_bank[:].rearrange("d (b l) -> d b l", l=L))
 
-        word_sum = held.tile([D, B], F32, name="word_sum")
-        nc.vector.reduce_sum(word_sum[:], x_words, axis=X_AXIS)
-        products = held.tile([D, B, L], BF16, name="products")
-        nc.vector.tensor_tensor(products[:], y_words, word_sum[:].unsqueeze(2).to_broadcast([D, B, L]), ALU.mult)
-        score_bank = banks.tile([P, N], F32, name="score_bank")
-        nc.tensor.matmul(score_bank[:], mean_weights[:], products[:].rearrange("d b l -> d (b l)"), start=True, stop=True)
-        scores = score_bank[:].rearrange("p (b l) -> p b l", l=L)
+            scores = []
+            for h in range(PIECES):
+                word_sum = work.tile([D, PIECE_B], F32, name="word_sum")
+                nc.vector.reduce_sum(word_sum[:], x_words[h], axis=X_AXIS)
+                products = work.tile([D, PIECE_B, L], BF16, name="products")
+                nc.vector.tensor_tensor(
+                    products[:], y_words[h], word_sum[:].unsqueeze(2).to_broadcast([D, PIECE_B, L]), ALU.mult
+                )
+                score_bank = banks.tile([P, PIECE_N], F32, name="score_bank")
+                nc.tensor.matmul(
+                    score_bank[:], mean_weights[:], products[:].rearrange("d b l -> d (b l)"), start=True, stop=True
+                )
+                scores.append(score_bank[:].rearrange("p (b l) -> p b l", l=L))
 
-        top = held.tile([P, B], F32, name="top")
-        nc.vector.reduce_max(top[:], scores, axis=X_AXIS)
-        shifted = held.tile([P, B, L], F32, name="shifted")
-        nc.vector.tensor_tensor(shifted[:], scores, top[:].unsqueeze(2).to_broadcast([P, B, L]), ALU.subtract)
-        grown = held.tile([P, B, L], F32, name="grown")
-        nc.scalar.activation(grown[:], shifted[:], EXP)
-        denominator = held.tile([P, B], F32, name="denominator")
-        nc.vector.reduce_sum(denominator[:], grown[:], axis=X_AXIS)
-        weighted = held.tile([D, B, L], F32, name="weighted")
-        nc.vector.tensor_tensor(weighted[:], x_words, grown[:], ALU.mult)
-        numerator = held.tile([D, B], F32, name="numerator")
-        nc.vector.reduce_sum(numerator[:], weighted[:], axis=X_AXIS)
-        inverse = held.tile([P, B], F32, name="inverse")
-        nc.vector.reciprocal(inverse[:], denominator[:])
-        result = held.tile([D, B], F32, name="result")
-        nc.vector.tensor_tensor(result[:], numerator[:], inverse[:], ALU.mult)
-        nc.sync.dma_start(out, result[:])
+            grown_words = []
+            for h in range(PIECES):
+                top = work.tile([P, PIECE_B], F32, name="top")
+                nc.vector.reduce_max(top[:], scores[h], axis=X_AXIS)
+                shifted = work.tile([P, PIECE_B, L], F32, name="shifted")
+                nc.vector.tensor_tensor(
+                    shifted[:], scores[h], top[:].unsqueeze(2).to_broadcast([P, PIECE_B, L]), ALU.subtract
+                )
+                grown = work.tile([P, PIECE_B, L], F32, name="grown")
+                nc.scalar.activation(grown[:], shifted[:], EXP)
+                grown_words.append(grown)
+
+            numerator = held.tile([D, B], F32, name="numerator")
+            denominator = held.tile([P, B], F32, name="denominator")
+            for h in range(PIECES):
+                sentences = slice(h * PIECE_B, (h + 1) * PIECE_B)
+                weighted = work.tile([D, PIECE_B, L], F32, name="weighted")
+                nc.vector.tensor_tensor(weighted[:], x_words[h], grown_words[h][:], ALU.mult)
+                nc.vector.reduce_sum(numerator[:, sentences], weighted[:], axis=X_AXIS)
+                nc.vector.reduce_sum(denominator[:, sentences], grown_words[h][:], axis=X_AXIS)
+            inverse = held.tile([P, B], F32, name="inverse")
+            nc.vector.reciprocal(inverse[:], denominator[:])
+            result = held.tile([D, B], F32, name="result")
+            nc.vector.tensor_tensor(result[:], numerator[:], inverse[:], ALU.mult)
+            nc.sync.dma_start(out, result[:])

@@ -10,9 +10,11 @@ P = 128
 V, D = 4096, 128
 B, L = 16, 32
 N = B * L
-PART_BLOCKS = 4
-PART = P * PART_BLOCKS
-PARTS = V // PART
+UNIT_BLOCKS = 4
+UNIT = P * UNIT_BLOCKS
+UNITS = V // UNIT
+LOAD_UNITS = 2
+LOADS = UNITS // LOAD_UNITS
 PIECES = 2
 PIECE_B = B // PIECES
 PIECE_N = N // PIECES
@@ -25,18 +27,17 @@ def tile_student_hyp_rec_kernel(tc, table, w, offs, out):
     nc = tc.nc
     with (
         tc.tile_pool(name="held", bufs=1) as held,
-        tc.tile_pool(name="rows", bufs=PARTS) as rows_pool,
+        tc.tile_pool(name="rows", bufs=LOADS) as rows_pool,
         tc.tile_pool(name="work", bufs=PIECES) as work,
     ):
-        table_blocks = table.rearrange("(k p) d -> p k d", p=P)
+        table_units = table.rearrange("(u p r) d -> p u (r d)", p=P, r=UNIT_BLOCKS)
         weights = held.tile([D, D], BF16, name="weights")
         nc.scalar.dma_start(weights[:], w)
-        parts = []
-        for g in range(PARTS):
-            rows = rows_pool.tile([P, PART_BLOCKS, D], BF16, name="rows")
-            queue = nc.sync if g % 2 == 0 else nc.scalar
-            queue.dma_start(rows[:], table_blocks[:, g * PART_BLOCKS : (g + 1) * PART_BLOCKS, :])
-            parts.append(rows)
+        loads = []
+        for g in range(LOADS):
+            rows = rows_pool.tile([P, LOAD_UNITS, UNIT_BLOCKS * D], BF16, name="rows")
+            nc.sync.dma_start(rows[:], table_units[:, g * LOAD_UNITS : (g + 1) * LOAD_UNITS, :])
+            loads.append(rows)
         offsets = held.tile([P, N // 16], U16, name="offsets")
         nc.sync.dma_start(offsets[:], offs)
 
@@ -51,15 +52,19 @@ def tile_student_hyp_rec_kernel(tc, table, w, offs, out):
 
         table_cols = held.tile([D, V], BF16, name="table_cols")
         with tc.psum_pool(name="flip", bufs=4) as flip_pool:
-            for g in range(PARTS):
-                flipped = flip_pool.tile([D, PART], BF16, name="flipped")
-                for k in range(PART_BLOCKS):
-                    nc.tensor.transpose(flipped[:, k * P : (k + 1) * P], parts[g][:, k, :], identity[:])
-                part_cols = table_cols[:, g * PART : (g + 1) * PART]
-                if g % 2 == 0:
-                    nc.scalar.copy(part_cols, flipped[:])
+            for u in range(UNITS):
+                rows = loads[u // LOAD_UNITS]
+                flipped = flip_pool.tile([D, UNIT], BF16, name="flipped")
+                for r in range(UNIT_BLOCKS):
+                    nc.tensor.transpose(
+                        flipped[:, r * P : (r + 1) * P], rows[:, u % LOAD_UNITS, r * D : (r + 1) * D], identity[:]
+                    )
+                unit_cols = table_cols[:, u * UNIT : (u + 1) * UNIT].rearrange("d (p r) -> d p r", r=UNIT_BLOCKS)
+                in_word_order = flipped[:].rearrange("d (r p) -> d p r", r=UNIT_BLOCKS)
+                if u % 2 == 0:
+                    nc.scalar.copy(unit_cols, in_word_order)
                 else:
-                    nc.vector.tensor_copy(part_cols, flipped[:])
+                    nc.vector.tensor_copy(unit_cols, in_word_order)
 
         with tc.psum_pool(name="banks", bufs=PIECES) as banks:
             x_words, y_words = [], []

@@ -15,6 +15,7 @@ UNIT = P * UNIT_BLOCKS
 UNITS = V // UNIT
 LOAD_UNITS = 2
 LOADS = UNITS // LOAD_UNITS
+WARM_MATMULS = 16
 PIECES = 2
 PIECE_B = B // PIECES
 PIECE_N = N // PIECES
@@ -41,17 +42,20 @@ def tile_student_hyp_rec_kernel(tc, table, w, offs, out):
         offsets = held.tile([P, N // 16], U16, name="offsets")
         nc.sync.dma_start(offsets[:], offs)
 
+        mean_weights = held.tile([D, P], BF16, name="mean_weights")
+        nc.vector.memset(mean_weights[:], 1.0 / L)
+        identity = held.tile([P, P], BF16, name="identity")
+        make_identity(nc, identity[:])
+
         scratch = held.tile([P, 1], F32, name="scratch")
         nc.vector.memset(scratch[:], 0.0)
         nc.scalar.activation(scratch[:], scratch[:], EXP)
 
-        identity = held.tile([P, P], BF16, name="identity")
-        make_identity(nc, identity[:])
-        mean_weights = held.tile([D, P], BF16, name="mean_weights")
-        nc.vector.memset(mean_weights[:], 1.0 / L)
-
         table_cols = held.tile([D, V], BF16, name="table_cols")
-        with tc.psum_pool(name="flip", bufs=4) as flip_pool:
+        with tc.psum_pool(name="warm", bufs=1) as warm_pool, tc.psum_pool(name="flip", bufs=4) as flip_pool:
+            warm_bank = warm_pool.tile([P, P], F32, name="warm_bank")
+            for i in range(WARM_MATMULS):
+                nc.tensor.matmul(warm_bank[:], mean_weights[:], mean_weights[:], start=True, stop=True)
             for u in range(UNITS):
                 rows = loads[u // LOAD_UNITS]
                 flipped = flip_pool.tile([D, UNIT], BF16, name="flipped")

@@ -16,7 +16,7 @@ UNITS = V // UNIT
 LOAD_UNITS = 2
 LOADS = UNITS // LOAD_UNITS
 WARM_MATMULS = 16
-PIECES = 2
+PIECES = 4
 PIECE_B = B // PIECES
 PIECE_N = N // PIECES
 PIECE_COLS = PIECE_N // 16
@@ -71,52 +71,57 @@ def tile_student_hyp_rec_kernel(tc, table, w, offs, out):
                     nc.vector.tensor_copy(unit_cols, in_word_order)
 
         with tc.psum_pool(name="banks", bufs=PIECES) as banks:
+
             x_words, y_words = [], []
             for h in range(PIECES):
                 piece = offsets[:, h * PIECE_COLS : (h + 1) * PIECE_COLS]
                 x_bank = banks.tile([D, PIECE_N], F32, name="x_bank")
                 nc.tensor.matmul(x_bank[:], identity[:], table_cols[:].indirect(piece), start=True, stop=True)
+                x_words.append(x_bank[:].rearrange("d (b l) -> d b l", l=L))
+            for h in range(PIECES):
+                piece = offsets[:, h * PIECE_COLS : (h + 1) * PIECE_COLS]
                 y_bank = banks.tile([D, PIECE_N], F32, name="y_bank")
                 nc.tensor.matmul(y_bank[:], weights[:], table_cols[:].indirect(piece), start=True, stop=True)
-                x_words.append(x_bank[:].rearrange("d (b l) -> d b l", l=L))
                 y_words.append(y_bank[:].rearrange("d (b l) -> d b l", l=L))
 
+            word_sum = held.tile([D, B], F32, name="word_sum")
+            for h in range(PIECES):
+                nc.vector.reduce_sum(word_sum[:, h * PIECE_B : (h + 1) * PIECE_B], x_words[h], axis=X_AXIS)
             scores = []
             for h in range(PIECES):
-                word_sum = work.tile([D, PIECE_B], F32, name="word_sum")
-                nc.vector.reduce_sum(word_sum[:], x_words[h], axis=X_AXIS)
+                piece_sum = word_sum[:, h * PIECE_B : (h + 1) * PIECE_B]
                 products = work.tile([D, PIECE_B, L], BF16, name="products")
                 nc.vector.tensor_tensor(
-                    products[:], y_words[h], word_sum[:].unsqueeze(2).to_broadcast([D, PIECE_B, L]), ALU.mult
+                    products[:], y_words[h], piece_sum.unsqueeze(2).to_broadcast([D, PIECE_B, L]), ALU.mult
                 )
-                score_bank = banks.tile([P, PIECE_N], F32, name="score_bank")
+                score_bank = banks.tile([P, PIECE_N], F32, name="score_bank", tag="y_bank")
                 nc.tensor.matmul(
                     score_bank[:], mean_weights[:], products[:].rearrange("d b l -> d (b l)"), start=True, stop=True
                 )
                 scores.append(score_bank[:].rearrange("p (b l) -> p b l", l=L))
 
-            grown_words = []
+            top = held.tile([P, B], F32, name="top")
             for h in range(PIECES):
-                top = work.tile([P, PIECE_B], F32, name="top")
-                nc.vector.reduce_max(top[:], scores[h], axis=X_AXIS)
+                nc.vector.reduce_max(top[:, h * PIECE_B : (h + 1) * PIECE_B], scores[h], axis=X_AXIS)
+            grown = held.tile([P, B, L], F32, name="grown")
+            for h in range(PIECES):
+                piece_top = top[:, h * PIECE_B : (h + 1) * PIECE_B]
                 shifted = work.tile([P, PIECE_B, L], F32, name="shifted")
                 nc.vector.tensor_tensor(
-                    shifted[:], scores[h], top[:].unsqueeze(2).to_broadcast([P, PIECE_B, L]), ALU.subtract
+                    shifted[:], scores[h], piece_top.unsqueeze(2).to_broadcast([P, PIECE_B, L]), ALU.subtract
                 )
-                grown = work.tile([P, PIECE_B, L], F32, name="grown")
-                nc.scalar.activation(grown[:], shifted[:], EXP)
-                grown_words.append(grown)
+                nc.scalar.activation(grown[:, h * PIECE_B : (h + 1) * PIECE_B, :], shifted[:], EXP)
 
-            numerator = held.tile([D, B], F32, name="numerator")
+            weighted = held.tile([D, B, L], F32, name="weighted")
             denominator = held.tile([P, B], F32, name="denominator")
             for h in range(PIECES):
                 sentences = slice(h * PIECE_B, (h + 1) * PIECE_B)
-                weighted = work.tile([D, PIECE_B, L], F32, name="weighted")
-                nc.vector.tensor_tensor(weighted[:], x_words[h], grown_words[h][:], ALU.mult)
-                nc.vector.reduce_sum(numerator[:, sentences], weighted[:], axis=X_AXIS)
-                nc.vector.reduce_sum(denominator[:, sentences], grown_words[h][:], axis=X_AXIS)
+                nc.vector.tensor_tensor(weighted[:, sentences, :], x_words[h], grown[:, sentences, :], ALU.mult)
+                nc.vector.reduce_sum(denominator[:, sentences], grown[:, sentences, :], axis=X_AXIS)
             inverse = held.tile([P, B], F32, name="inverse")
             nc.vector.reciprocal(inverse[:], denominator[:])
+            numerator = held.tile([D, B], F32, name="numerator")
+            nc.vector.reduce_sum(numerator[:], weighted[:], axis=X_AXIS)
             result = held.tile([D, B], F32, name="result")
             nc.vector.tensor_tensor(result[:], numerator[:], inverse[:], ALU.mult)
             nc.sync.dma_start(out, result[:])

@@ -43,7 +43,7 @@ def tile_student_hyp_rec_kernel(tc, table, w, offs, out):
         nc.sync.dma_start(offsets[:], offs)
 
         mean_weights = held.tile([D, P], BF16, name="mean_weights")
-        nc.vector.memset(mean_weights[:], 1.0 / L)
+        nc.vector.memset(mean_weights[:], -1.0 / L)
         identity = held.tile([P, P], BF16, name="identity")
         make_identity(nc, identity[:])
 
@@ -100,24 +100,25 @@ def tile_student_hyp_rec_kernel(tc, table, w, offs, out):
                 )
                 scores.append(score_bank[:].rearrange("p (b l) -> p b l", l=L))
 
-            top = held.tile([P, B], F32, name="top")
+            minus_top = held.tile([P, B], F32, name="minus_top")
             for h in range(PIECES):
-                nc.vector.reduce_max(top[:, h * PIECE_B : (h + 1) * PIECE_B], scores[h], axis=X_AXIS)
+                nc.vector.tensor_reduce(minus_top[:, h * PIECE_B : (h + 1) * PIECE_B], scores[h], axis=X_AXIS, op=ALU.min)
             grown = held.tile([P, B, L], F32, name="grown")
-            for h in range(PIECES):
-                piece_top = top[:, h * PIECE_B : (h + 1) * PIECE_B]
-                shifted = work.tile([P, PIECE_B, L], F32, name="shifted")
-                nc.vector.tensor_tensor(
-                    shifted[:], scores[h], piece_top.unsqueeze(2).to_broadcast([P, PIECE_B, L]), ALU.subtract
+            denominator = held.tile([P, B], F32, name="denominator")
+            for b in range(B):
+                nc.scalar.activation(
+                    grown[:, b, :],
+                    scores[b // PIECE_B][:, b % PIECE_B, :],
+                    EXP,
+                    bias=minus_top[:, b : b + 1],
+                    scale=-1.0,
+                    accum_out=denominator[:, b : b + 1],
                 )
-                nc.scalar.activation(grown[:, h * PIECE_B : (h + 1) * PIECE_B, :], shifted[:], EXP)
 
             weighted = held.tile([D, B, L], F32, name="weighted")
-            denominator = held.tile([P, B], F32, name="denominator")
             for h in range(PIECES):
                 sentences = slice(h * PIECE_B, (h + 1) * PIECE_B)
                 nc.vector.tensor_tensor(weighted[:, sentences, :], x_words[h], grown[:, sentences, :], ALU.mult)
-                nc.vector.reduce_sum(denominator[:, sentences], grown[:, sentences, :], axis=X_AXIS)
             inverse = held.tile([P, B], F32, name="inverse")
             nc.vector.reciprocal(inverse[:], denominator[:])
             numerator = held.tile([D, B], F32, name="numerator")

@@ -115,14 +115,14 @@ def tile_student_hyp_rec_kernel(tc, table, w, offs, out):
                     accum_out=denominator[:, b : b + 1],
                 )
 
-            weighted = held.tile([D, B, L], F32, name="weighted")
+            inverse = held.tile([P, B], F32, name="inverse")
+            numerator = held.tile([D, B], F32, name="numerator")
             for h in range(PIECES):
                 sentences = slice(h * PIECE_B, (h + 1) * PIECE_B)
-                nc.vector.tensor_tensor(weighted[:, sentences, :], x_words[h], grown[:, sentences, :], ALU.mult)
-            inverse = held.tile([P, B], F32, name="inverse")
-            nc.vector.reciprocal(inverse[:], denominator[:])
-            numerator = held.tile([D, B], F32, name="numerator")
-            nc.vector.reduce_sum(numerator[:], weighted[:], axis=X_AXIS)
+                weighted = work.tile([D, PIECE_B, L], F32, name="weighted")
+                nc.vector.tensor_tensor(weighted[:], x_words[h], grown[:, sentences, :], ALU.mult)
+                nc.vector.reciprocal(inverse[:, sentences], denominator[:, sentences])
+                nc.vector.reduce_sum(numerator[:, sentences], weighted[:], axis=X_AXIS)
             result = held.tile([D, B], F32, name="result")
             nc.vector.tensor_tensor(result[:], numerator[:], inverse[:], ALU.mult)
             nc.sync.dma_start(out, result[:])

@@ -117,12 +117,18 @@ def tile_student_hyp_rec_kernel(tc, table, w, offs, out):
 
             inverse = held.tile([P, B], F32, name="inverse")
             numerator = held.tile([D, B], F32, name="numerator")
-            for h in range(PIECES):
-                sentences = slice(h * PIECE_B, (h + 1) * PIECE_B)
+            chunk_starts = list(range(0, B - PIECE_B, PIECE_B)) + [B - PIECE_B, B - PIECE_B // 2]
+            for first, end in zip(chunk_starts, chunk_starts[1:] + [B]):
+                h = first // PIECE_B
                 weighted = work.tile([D, PIECE_B, L], F32, name="weighted")
-                nc.vector.tensor_tensor(weighted[:], x_words[h], grown[:, sentences, :], ALU.mult)
-                nc.vector.reciprocal(inverse[:, sentences], denominator[:, sentences])
-                nc.vector.reduce_sum(numerator[:, sentences], weighted[:], axis=X_AXIS)
+                nc.vector.tensor_tensor(
+                    weighted[:, : end - first, :],
+                    x_words[h][:, first - h * PIECE_B : end - h * PIECE_B, :],
+                    grown[:, first:end, :],
+                    ALU.mult,
+                )
+                nc.vector.reduce_sum(numerator[:, first:end], weighted[:, : end - first, :], axis=X_AXIS)
+            nc.vector.reciprocal(inverse[:], denominator[:])
             result = held.tile([D, B], F32, name="result")
             nc.vector.tensor_tensor(result[:], numerator[:], inverse[:], ALU.mult)
             nc.sync.dma_start(out, result[:])

import concourse.mybir as mybir
from concourse.masks import make_identity

BF16, F32, U16 = mybir.dt.bfloat16, mybir.dt.float32, mybir.dt.uint16
ALU = mybir.AluOpType
X_AXIS = mybir.AxisListType.X
EXP = mybir.ActivationFunctionType.Exp

P = 128
V, D = 4096, 128
B, L = 16, 32
N = B * L
UNIT_BLOCKS = 4
UNIT = P * UNIT_BLOCKS
UNITS = V // UNIT
LOAD_UNITS = 2
LOADS = UNITS // LOAD_UNITS
WARM_MATMULS = 16
PIECES = 4
PIECE_B = B // PIECES
PIECE_N = N // PIECES
PIECE_COLS = PIECE_N // 16

FLOPS = 2 * D * D * N + 4 * D * N


def tile_student_hyp_rec_kernel(tc, table, w, offs, out):
    nc = tc.nc
    with (
        tc.tile_pool(name="held", bufs=1) as held,
        tc.tile_pool(name="rows", bufs=LOADS) as rows_pool,
        tc.tile_pool(name="work", bufs=PIECES) as work,
    ):
        table_units = table.rearrange("(u p r) d -> p u (r d)", p=P, r=UNIT_BLOCKS)
        weights = held.tile([D, D], BF16, name="weights")
        nc.scalar.dma_start(weights[:], w)
        loads = []
        for g in range(LOADS):
            rows = rows_pool.tile([P, LOAD_UNITS, UNIT_BLOCKS * D], BF16, name="rows")
            nc.sync.dma_start(rows[:], table_units[:, g * LOAD_UNITS : (g + 1) * LOAD_UNITS, :])
            loads.append(rows)
        offsets = held.tile([P, N // 16], U16, name="offsets")
        nc.sync.dma_start(offsets[:], offs)

        mean_weights = held.tile([D, P], BF16, name="mean_weights")
        nc.vector.memset(mean_weights[:], -1.0 / L)
        identity = held.tile([P, P], BF16, name="identity")
        make_identity(nc, identity[:])

        scratch = held.tile([P, 1], F32, name="scratch")
        nc.vector.memset(scratch[:], 0.0)
        nc.scalar.activation(scratch[:], scratch[:], EXP)

        table_cols = held.tile([D, V], BF16, name="table_cols")
        with tc.psum_pool(name="warm", bufs=1) as warm_pool, tc.psum_pool(name="flip", bufs=4) as flip_pool:
            warm_bank = warm_pool.tile([P, P], F32, name="warm_bank")
            for i in range(WARM_MATMULS):
                nc.tensor.matmul(warm_bank[:], mean_weights[:], mean_weights[:], start=True, stop=True)
            for u in range(UNITS):
                rows = loads[u // LOAD_UNITS]
                flipped = flip_pool.tile([D, UNIT], BF16, name="flipped")
                for r in range(UNIT_BLOCKS):
                    nc.tensor.transpose(
                        flipped[:, r * P : (r + 1) * P], rows[:, u % LOAD_UNITS, r * D : (r + 1) * D], identity[:]
                    )
                unit_cols = table_cols[:, u * UNIT : (u + 1) * UNIT].rearrange("d (p r) -> d p r", r=UNIT_BLOCKS)
                in_word_order = flipped[:].rearrange("d (r p) -> d p r", r=UNIT_BLOCKS)
                if u % 2 == 0:
                    nc.scalar.copy(unit_cols, in_word_order)
                else:
                    nc.vector.tensor_copy(unit_cols, in_word_order)

        with tc.psum_pool(name="banks", bufs=PIECES) as banks:

            x_words, y_words = [], []
            for h in range(PIECES):
                piece = offsets[:, h * PIECE_COLS : (h + 1) * PIECE_COLS]
                x_bank = banks.tile([D, PIECE_N], F32, name="x_bank")
                nc.tensor.matmul(x_bank[:], identity[:], table_cols[:].indirect(piece), start=True, stop=True)
                x_words.append(x_bank[:].rearrange("d (b l) -> d b l", l=L))
            for h in range(PIECES):
                piece = offsets[:, h * PIECE_COLS : (h + 1) * PIECE_COLS]
                y_bank = banks.tile([D, PIECE_N], F32, name="y_bank")
                nc.tensor.matmul(y_bank[:], weights[:], table_cols[:].indirect(piece), start=True, stop=True)
                y_words.append(y_bank[:].rearrange("d (b l) -> d b l", l=L))

            word_sum = held.tile([D, B], F32, name="word_sum")
            for h in range(PIECES):
                nc.vector.reduce_sum(word_sum[:, h * PIECE_B : (h + 1) * PIECE_B], x_words[h], axis=X_AXIS)
            scores = []
            for h in range(PIECES):
                piece_sum = word_sum[:, h * PIECE_B : (h + 1) * PIECE_B]
                products = work.tile([D, PIECE_B, L], BF16, name="products")
                nc.vector.tensor_tensor(
                    products[:], y_words[h], piece_sum.unsqueeze(2).to_broadcast([D, PIECE_B, L]), ALU.mult
                )
                score_bank = banks.tile([P, PIECE_N], F32, name="score_bank", tag="y_bank")
                nc.tensor.matmul(
                    score_bank[:], mean_weights[:], products[:].rearrange("d b l -> d (b l)"), start=True, stop=True
                )
                scores.append(score_bank[:].rearrange("p (b l) -> p b l", l=L))

            minus_top = held.tile([P, B], F32, name="minus_top")
            for h in range(PIECES):
                nc.vector.tensor_reduce(minus_top[:, h * PIECE_B : (h + 1) * PIECE_B], scores[h], axis=X_AXIS, op=ALU.min)
            grown = held.tile([P, B, L], F32, name="grown")
            denominator = held.tile([P, B], F32, name="denominator")
            for b in range(B):
                nc.scalar.activation(
                    grown[:, b, :],
                    scores[b // PIECE_B][:, b % PIECE_B, :],
                    EXP,
                    bias=minus_top[:, b : b + 1],
                    scale=-1.0,
                    accum_out=denominator[:, b : b + 1],
                )

            inverse = held.tile([P, B], F32, name="inverse")
            numerator = held.tile([D, B], F32, name="numerator")
            chunk_starts = list(range(0, B - PIECE_B, PIECE_B)) + [B - PIECE_B, B - PIECE_B // 2]
            for first, end in zip(chunk_starts, chunk_starts[1:] + [B]):
                h = first // PIECE_B
                weighted = work.tile([D, PIECE_B, L], F32, name="weighted")
                nc.vector.tensor_tensor(
                    weighted[:, : end - first, :],
                    x_words[h][:, first - h * PIECE_B : end - h * PIECE_B, :],
                    grown[:, first:end, :],
                    ALU.mult,
                )
                nc.vector.reduce_sum(numerator[:, first:end], weighted[:, : end - first, :], axis=X_AXIS)
            nc.vector.reciprocal(inverse[:], denominator[:])
            result = held.tile([D, B], F32, name="result")
            nc.vector.tensor_tensor(result[:], numerator[:], inverse[:], ALU.mult)
            nc.sync.dma_start(out, result[:])
